import numpy as np
import ml_dtypes

BF16 = ml_dtypes.bfloat16


def bf(x):
    return np.asarray(x, np.float32).astype(BF16)


def f32(x):
    return np.asarray(x, np.float32)


def f64(x):
    return np.asarray(x).astype(np.float64)


def striped(idx):
    return np.tile(idx.reshape(-1, 16).T, (8, 1))


V, D, T, K, N = 512, 128, 128, 8, 1024


def setup_inputs():
    return {"table": bf(np.random.standard_normal((V, D))), "latent": bf(np.random.standard_normal((D, T)) / np.sqrt(D)), "offs": striped(np.random.permutation(np.tile(np.arange(V), 2))[:N])}


def reference(table, latent, offs):
    idx = offs[:16].T.reshape(-1)
    score = f64(latent).T @ f64(table)[idx].T
    sc = score.reshape(T, T, K)
    return sc[:, :, K - 1] - np.log(np.exp(sc).sum(axis=2))

@@ -1,0 +1,71 @@
+import concourse.mybir as mybir
+from concourse.masks import make_identity
+
+BF16, F32, U16 = mybir.dt.bfloat16, mybir.dt.float32, mybir.dt.uint16
+ALU = mybir.AluOpType
+ACT = mybir.ActivationFunctionType
+X = mybir.AxisListType.X
+
+P = 128
+V, D, T, K, N = 512, 128, 128, 8, 1024
+BLOCKS = V // P
+PIECE = 512
+TARGETS = PIECE // K
+
+FLOPS = 2 * T * D * N
+
+
+def tile_neg_loss_kernel(tc, table, latent, offs, out):
+    nc = tc.nc
+    with (
+        tc.tile_pool(name="held", bufs=1) as held,
+        tc.tile_pool(name="work", bufs=2) as work,
+        tc.psum_pool(name="flip", bufs=2) as flip,
+        tc.psum_pool(name="banks", bufs=2) as banks,
+    ):
+        offsets = held.tile([P, N // 16], U16, name="offsets")
+        nc.sync.dma_start(offsets[:], offs)
+        weights = held.tile([D, T], BF16, name="weights")
+        nc.sync.dma_start(weights[:], latent)
+        words = held.tile([P, BLOCKS, D], BF16, name="words")
+        nc.scalar.dma_start(words[:], table.rearrange("(b p) d -> p b d", p=P))
+
+        identity = held.tile([P, P], BF16, name="identity")
+        make_identity(nc, identity[:])
+
+        window = held.tile([D, V], BF16, name="window")
+        for b in range(BLOCKS):
+            flipped = flip.tile([D, P], BF16, name="flipped")
+            nc.tensor.transpose(flipped[:], words[:, b, :], identity[:])
+            nc.vector.tensor_copy(window[:, b * P : (b + 1) * P], flipped[:])
+
+        result = held.tile([T, T], F32, name="result")
+        for piece in range(N // PIECE):
+            columns = slice(piece * (PIECE // 16), (piece + 1) * (PIECE // 16))
+            score = banks.tile([T, TARGETS, K], F32, name="score")
+            nc.tensor.matmul(
+                score[:].rearrange("m t q -> m (t q)"),
+                weights[:],
+                window[:].indirect(offsets[:, columns]),
+                start=True,
+                stop=True,
+            )
+            top = work.tile([T, TARGETS], F32, name="top")
+            nc.vector.tensor_reduce(top[:], score[:], axis=X, op=ALU.max)
+            shifted = work.tile([T, TARGETS, K], F32, name="shifted")
+            nc.vector.tensor_tensor(
+                shifted[:], score[:], top[:].unsqueeze(2).to_broadcast([T, TARGETS, K]), ALU.subtract
+            )
+            powers = work.tile([T, TARGETS, K], F32, name="powers")
+            nc.scalar.activation(powers[:], shifted[:], ACT.Exp)
+            total = work.tile([T, TARGETS], F32, name="total")
+            nc.vector.tensor_reduce(total[:], powers[:], axis=X, op=ALU.add)
+            log_total = work.tile([T, TARGETS], F32, name="log_total")
+            nc.scalar.activation(log_total[:], total[:], ACT.Ln)
+            nc.vector.tensor_tensor(
+                result[:, piece * TARGETS : (piece + 1) * TARGETS],
+                shifted[:, :, K - 1],
+                log_total[:],
+                ALU.subtract,
+            )
+        nc.sync.dma_start(out, result[:])

@@ -10,6 +10,7 @@ P = 128
 V, D, T, K, N = 512, 128, 128, 8, 1024
 BLOCKS = V // P
 PIECE = 512
+PIECES = N // PIECE
 TARGETS = PIECE // K
 
 FLOPS = 2 * T * D * N
@@ -19,9 +20,8 @@ def tile_neg_loss_kernel(tc, table, latent, offs, out):
     nc = tc.nc
     with (
         tc.tile_pool(name="held", bufs=1) as held,
-        tc.tile_pool(name="work", bufs=2) as work,
         tc.psum_pool(name="flip", bufs=2) as flip,
-        tc.psum_pool(name="banks", bufs=2) as banks,
+        tc.psum_pool(name="banks", bufs=PIECES) as banks,
     ):
         offsets = held.tile([P, N // 16], U16, name="offsets")
         nc.sync.dma_start(offsets[:], offs)
@@ -33,15 +33,26 @@ def tile_neg_loss_kernel(tc, table, latent, offs, out):
         identity = held.tile([P, P], BF16, name="identity")
         make_identity(nc, identity[:])
 
+        early = held.tile([P, 1], F32, name="early")
+        nc.vector.memset(early[:], 0.0)
+        nc.scalar.activation(early[:], early[:], ACT.Exp)
+
         window = held.tile([D, V], BF16, name="window")
         for b in range(BLOCKS):
             flipped = flip.tile([D, P], BF16, name="flipped")
             nc.tensor.transpose(flipped[:], words[:, b, :], identity[:])
             nc.vector.tensor_copy(window[:, b * P : (b + 1) * P], flipped[:])
 
+        top = held.tile([T, T], F32, name="top")
+        shifted = held.tile([T, T, K], F32, name="shifted")
+        powers = held.tile([T, T, K], F32, name="powers")
+        total = held.tile([T, T], F32, name="total")
+        log_total = held.tile([T, T], F32, name="log_total")
         result = held.tile([T, T], F32, name="result")
-        for piece in range(N // PIECE):
+
+        for piece in range(PIECES):
             columns = slice(piece * (PIECE // 16), (piece + 1) * (PIECE // 16))
+            targets = slice(piece * TARGETS, (piece + 1) * TARGETS)
             score = banks.tile([T, TARGETS, K], F32, name="score")
             nc.tensor.matmul(
                 score[:].rearrange("m t q -> m (t q)"),
@@ -50,22 +61,17 @@ def tile_neg_loss_kernel(tc, table, latent, offs, out):
                 start=True,
                 stop=True,
             )
-            top = work.tile([T, TARGETS], F32, name="top")
-            nc.vector.tensor_reduce(top[:], score[:], axis=X, op=ALU.max)
-            shifted = work.tile([T, TARGETS, K], F32, name="shifted")
+            nc.vector.tensor_reduce(top[:, targets], score[:], axis=X, op=ALU.max)
             nc.vector.tensor_tensor(
-                shifted[:], score[:], top[:].unsqueeze(2).to_broadcast([T, TARGETS, K]), ALU.subtract
-            )
-            powers = work.tile([T, TARGETS, K], F32, name="powers")
-            nc.scalar.activation(powers[:], shifted[:], ACT.Exp)
-            total = work.tile([T, TARGETS], F32, name="total")
-            nc.vector.tensor_reduce(total[:], powers[:], axis=X, op=ALU.add)
-            log_total = work.tile([T, TARGETS], F32, name="log_total")
-            nc.scalar.activation(log_total[:], total[:], ACT.Ln)
-            nc.vector.tensor_tensor(
-                result[:, piece * TARGETS : (piece + 1) * TARGETS],
-                shifted[:, :, K - 1],
-                log_total[:],
+                shifted[:, targets, :],
+                score[:],
+                top[:, targets].unsqueeze(2).to_broadcast([T, TARGETS, K]),
                 ALU.subtract,
             )
+            nc.scalar.activation(powers[:, targets, :], shifted[:, targets, :], ACT.Exp)
+        for piece in range(PIECES):
+            targets = slice(piece * TARGETS, (piece + 1) * TARGETS)
+            nc.vector.tensor_reduce(total[:, targets], powers[:, targets, :], axis=X, op=ALU.add)
+        nc.scalar.activation(log_total[:], total[:], ACT.Ln)
+        nc.vector.tensor_tensor(result[:], shifted[:, :, K - 1], log_total[:], ALU.subtract)
         nc.sync.dma_start(out, result[:])

@@ -12,6 +12,7 @@ BLOCKS = V // P
 PIECE = 512
 PIECES = N // PIECE
 TARGETS = PIECE // K
+WARMING = 4
 
 FLOPS = 2 * T * D * N
 
@@ -22,6 +23,7 @@ def tile_neg_loss_kernel(tc, table, latent, offs, out):
         tc.tile_pool(name="held", bufs=1) as held,
         tc.psum_pool(name="flip", bufs=2) as flip,
         tc.psum_pool(name="banks", bufs=PIECES) as banks,
+        tc.psum_pool(name="spare", bufs=1) as spare,
     ):
         offsets = held.tile([P, N // 16], U16, name="offsets")
         nc.sync.dma_start(offsets[:], offs)
@@ -29,6 +31,12 @@ def tile_neg_loss_kernel(tc, table, latent, offs, out):
         nc.sync.dma_start(weights[:], latent)
         words = held.tile([P, BLOCKS, D], BF16, name="words")
         nc.scalar.dma_start(words[:], table.rearrange("(b p) d -> p b d", p=P))
+
+        zeros = held.tile([P, PIECE], BF16, name="zeros")
+        nc.vector.memset(zeros[:], 0.0)
+        unread = spare.tile([P, PIECE], F32, name="unread")
+        for turn in range(WARMING):
+            nc.tensor.matmul(unread[:], zeros[:, :P], zeros[:], start=True, stop=True)
 
         identity = held.tile([P, P], BF16, name="identity")
         make_identity(nc, identity[:])

@@ -9,10 +9,9 @@ X = mybir.AxisListType.X
 P = 128
 V, D, T, K, N = 512, 128, 128, 8, 1024
 BLOCKS = V // P
-PIECE = 512
+PIECE = 256
 PIECES = N // PIECE
 TARGETS = PIECE // K
-WARMING = 4
 
 FLOPS = 2 * T * D * N
 
@@ -21,29 +20,20 @@ def tile_neg_loss_kernel(tc, table, latent, offs, out):
     nc = tc.nc
     with (
         tc.tile_pool(name="held", bufs=1) as held,
-        tc.psum_pool(name="flip", bufs=2) as flip,
+        tc.psum_pool(name="flip", bufs=BLOCKS) as flip,
         tc.psum_pool(name="banks", bufs=PIECES) as banks,
-        tc.psum_pool(name="spare", bufs=1) as spare,
     ):
+        words = held.tile([P, BLOCKS, D], BF16, name="words")
+        for b in range(BLOCKS):
+            queue = nc.sync if b % 2 == 0 else nc.scalar
+            queue.dma_start(words[:, b, :], table[b * P : (b + 1) * P, :])
         offsets = held.tile([P, N // 16], U16, name="offsets")
         nc.sync.dma_start(offsets[:], offs)
         weights = held.tile([D, T], BF16, name="weights")
-        nc.sync.dma_start(weights[:], latent)
-        words = held.tile([P, BLOCKS, D], BF16, name="words")
-        nc.scalar.dma_start(words[:], table.rearrange("(b p) d -> p b d", p=P))
-
-        zeros = held.tile([P, PIECE], BF16, name="zeros")
-        nc.vector.memset(zeros[:], 0.0)
-        unread = spare.tile([P, PIECE], F32, name="unread")
-        for turn in range(WARMING):
-            nc.tensor.matmul(unread[:], zeros[:, :P], zeros[:], start=True, stop=True)
+        nc.scalar.dma_start(weights[:], latent)
 
         identity = held.tile([P, P], BF16, name="identity")
         make_identity(nc, identity[:])
-
-        early = held.tile([P, 1], F32, name="early")
-        nc.vector.memset(early[:], 0.0)
-        nc.scalar.activation(early[:], early[:], ACT.Exp)
 
         window = held.tile([D, V], BF16, name="window")
         for b in range(BLOCKS):

@@ -21,7 +21,7 @@ def tile_neg_loss_kernel(tc, table, latent, offs, out):
     with (
         tc.tile_pool(name="held", bufs=1) as held,
         tc.psum_pool(name="flip", bufs=BLOCKS) as flip,
-        tc.psum_pool(name="banks", bufs=PIECES) as banks,
+        tc.psum_pool(name="banks", bufs=1) as banks,
     ):
         words = held.tile([P, BLOCKS, D], BF16, name="words")
         for b in range(BLOCKS):
@@ -48,25 +48,30 @@ def tile_neg_loss_kernel(tc, table, latent, offs, out):
         log_total = held.tile([T, T], F32, name="log_total")
         result = held.tile([T, T], F32, name="result")
 
+        scores = [banks.tile([T, TARGETS, K], F32, name=f"score{piece}") for piece in range(PIECES)]
         for piece in range(PIECES):
             columns = slice(piece * (PIECE // 16), (piece + 1) * (PIECE // 16))
-            targets = slice(piece * TARGETS, (piece + 1) * TARGETS)
-            score = banks.tile([T, TARGETS, K], F32, name="score")
             nc.tensor.matmul(
-                score[:].rearrange("m t q -> m (t q)"),
+                scores[piece][:].rearrange("m t q -> m (t q)"),
                 weights[:],
                 window[:].indirect(offsets[:, columns]),
                 start=True,
                 stop=True,
             )
-            nc.vector.tensor_reduce(top[:, targets], score[:], axis=X, op=ALU.max)
-            nc.vector.tensor_tensor(
-                shifted[:, targets, :],
-                score[:],
-                top[:, targets].unsqueeze(2).to_broadcast([T, TARGETS, K]),
-                ALU.subtract,
-            )
-            nc.scalar.activation(powers[:, targets, :], shifted[:, targets, :], ACT.Exp)
+
+        for step in range(PIECES + 1):
+            if step < PIECES:
+                targets = slice(step * TARGETS, (step + 1) * TARGETS)
+                nc.vector.tensor_reduce(top[:, targets], scores[step][:], axis=X, op=ALU.max)
+            if step > 0:
+                targets = slice((step - 1) * TARGETS, step * TARGETS)
+                nc.vector.tensor_tensor(
+                    shifted[:, targets, :],
+                    scores[step - 1][:],
+                    top[:, targets].unsqueeze(2).to_broadcast([T, TARGETS, K]),
+                    ALU.subtract,
+                )
+                nc.scalar.activation(powers[:, targets, :], shifted[:, targets, :], ACT.Exp)
         for piece in range(PIECES):
             targets = slice(piece * TARGETS, (piece + 1) * TARGETS)
             nc.vector.tensor_reduce(total[:, targets], powers[:, targets, :], axis=X, op=ALU.add)

@@ -21,7 +21,7 @@ def tile_neg_loss_kernel(tc, table, latent, offs, out):
     with (
         tc.tile_pool(name="held", bufs=1) as held,
         tc.psum_pool(name="flip", bufs=BLOCKS) as flip,
-        tc.psum_pool(name="banks", bufs=1) as banks,
+        tc.psum_pool(name="banks", bufs=PIECES) as banks,
     ):
         words = held.tile([P, BLOCKS, D], BF16, name="words")
         for b in range(BLOCKS):
@@ -39,7 +39,10 @@ def tile_neg_loss_kernel(tc, table, latent, offs, out):
         for b in range(BLOCKS):
             flipped = flip.tile([D, P], BF16, name="flipped")
             nc.tensor.transpose(flipped[:], words[:, b, :], identity[:])
-            nc.vector.tensor_copy(window[:, b * P : (b + 1) * P], flipped[:])
+            if b % 2 == 0:
+                nc.vector.tensor_copy(window[:, b * P : (b + 1) * P], flipped[:])
+            else:
+                nc.scalar.copy(window[:, b * P : (b + 1) * P], flipped[:])
 
         top = held.tile([T, T], F32, name="top")
         shifted = held.tile([T, T, K], F32, name="shifted")
@@ -48,30 +51,25 @@ def tile_neg_loss_kernel(tc, table, latent, offs, out):
         log_total = held.tile([T, T], F32, name="log_total")
         result = held.tile([T, T], F32, name="result")
 
-        scores = [banks.tile([T, TARGETS, K], F32, name=f"score{piece}") for piece in range(PIECES)]
         for piece in range(PIECES):
             columns = slice(piece * (PIECE // 16), (piece + 1) * (PIECE // 16))
+            targets = slice(piece * TARGETS, (piece + 1) * TARGETS)
+            score = banks.tile([T, TARGETS, K], F32, name="score")
             nc.tensor.matmul(
-                scores[piece][:].rearrange("m t q -> m (t q)"),
+                score[:].rearrange("m t q -> m (t q)"),
                 weights[:],
                 window[:].indirect(offsets[:, columns]),
                 start=True,
                 stop=True,
             )
-
-        for step in range(PIECES + 1):
-            if step < PIECES:
-                targets = slice(step * TARGETS, (step + 1) * TARGETS)
-                nc.vector.tensor_reduce(top[:, targets], scores[step][:], axis=X, op=ALU.max)
-            if step > 0:
-                targets = slice((step - 1) * TARGETS, step * TARGETS)
-                nc.vector.tensor_tensor(
-                    shifted[:, targets, :],
-                    scores[step - 1][:],
-                    top[:, targets].unsqueeze(2).to_broadcast([T, TARGETS, K]),
-                    ALU.subtract,
-                )
-                nc.scalar.activation(powers[:, targets, :], shifted[:, targets, :], ACT.Exp)
+            nc.vector.tensor_reduce(top[:, targets], score[:], axis=X, op=ALU.max)
+            nc.vector.tensor_tensor(
+                shifted[:, targets, :],
+                score[:],
+                top[:, targets].unsqueeze(2).to_broadcast([T, TARGETS, K]),
+                ALU.subtract,
+            )
+            nc.scalar.activation(powers[:, targets, :], shifted[:, targets, :], ACT.Exp)
         for piece in range(PIECES):
             targets = slice(piece * TARGETS, (piece + 1) * TARGETS)
             nc.vector.tensor_reduce(total[:, targets], powers[:, targets, :], axis=X, op=ALU.add)

import concourse.mybir as mybir
from concourse.masks import make_identity

BF16, F32, U16 = mybir.dt.bfloat16, mybir.dt.float32, mybir.dt.uint16
ALU = mybir.AluOpType
ACT = mybir.ActivationFunctionType
X = mybir.AxisListType.X

P = 128
V, D, T, K, N = 512, 128, 128, 8, 1024
BLOCKS = V // P
PIECE = 256
PIECES = N // PIECE
TARGETS = PIECE // K

FLOPS = 2 * T * D * N


def tile_neg_loss_kernel(tc, table, latent, offs, out):
    nc = tc.nc
    with (
        tc.tile_pool(name="held", bufs=1) as held,
        tc.psum_pool(name="flip", bufs=BLOCKS) as flip,
        tc.psum_pool(name="banks", bufs=PIECES) as banks,
    ):
        words = held.tile([P, BLOCKS, D], BF16, name="words")
        for b in range(BLOCKS):
            queue = nc.sync if b % 2 == 0 else nc.scalar
            queue.dma_start(words[:, b, :], table[b * P : (b + 1) * P, :])
        offsets = held.tile([P, N // 16], U16, name="offsets")
        nc.sync.dma_start(offsets[:], offs)
        weights = held.tile([D, T], BF16, name="weights")
        nc.scalar.dma_start(weights[:], latent)

        identity = held.tile([P, P], BF16, name="identity")
        make_identity(nc, identity[:])

        window = held.tile([D, V], BF16, name="window")
        for b in range(BLOCKS):
            flipped = flip.tile([D, P], BF16, name="flipped")
            nc.tensor.transpose(flipped[:], words[:, b, :], identity[:])
            if b % 2 == 0:
                nc.vector.tensor_copy(window[:, b * P : (b + 1) * P], flipped[:])
            else:
                nc.scalar.copy(window[:, b * P : (b + 1) * P], flipped[:])

        top = held.tile([T, T], F32, name="top")
        shifted = held.tile([T, T, K], F32, name="shifted")
        powers = held.tile([T, T, K], F32, name="powers")
        total = held.tile([T, T], F32, name="total")
        log_total = held.tile([T, T], F32, name="log_total")
        result = held.tile([T, T], F32, name="result")

        for piece in range(PIECES):
            columns = slice(piece * (PIECE // 16), (piece + 1) * (PIECE // 16))
            targets = slice(piece * TARGETS, (piece + 1) * TARGETS)
            score = banks.tile([T, TARGETS, K], F32, name="score")
            nc.tensor.matmul(
                score[:].rearrange("m t q -> m (t q)"),
                weights[:],
                window[:].indirect(offsets[:, columns]),
                start=True,
                stop=True,
            )
            nc.vector.tensor_reduce(top[:, targets], score[:], axis=X, op=ALU.max)
            nc.vector.tensor_tensor(
                shifted[:, targets, :],
                score[:],
                top[:, targets].unsqueeze(2).to_broadcast([T, TARGETS, K]),
                ALU.subtract,
            )
            nc.scalar.activation(powers[:, targets, :], shifted[:, targets, :], ACT.Exp)
        for piece in range(PIECES):
            targets = slice(piece * TARGETS, (piece + 1) * TARGETS)
            nc.vector.tensor_reduce(total[:, targets], powers[:, targets, :], axis=X, op=ALU.add)
        nc.scalar.activation(log_total[:], total[:], ACT.Ln)
        nc.vector.tensor_tensor(result[:], shifted[:, :, K - 1], log_total[:], ALU.subtract)
        nc.sync.dma_start(out, result[:])
